import numpy as np
import ml_dtypes


def mxq(x, axis, fmt="e4m3"):
    dtype, down = {"e4m3": (ml_dtypes.float8_e4m3fn, 7), "e5m2": (ml_dtypes.float8_e5m2, 14)}[fmt]
    v = np.moveaxis(np.asarray(x, np.float32).astype(ml_dtypes.bfloat16).astype(np.float64), axis, -1)
    blocks = v.reshape(v.shape[:-1] + (-1, 32))
    amax = np.abs(blocks).max(-1, keepdims=True)
    byte = np.maximum(np.where(amax > 0, np.frexp(amax)[1] - 1 + 127, 0) - down, 1)
    scale = np.exp2(byte - 127.0)
    codes = (blocks / scale).astype(np.float32).astype(dtype).astype(np.float64)
    return np.moveaxis((codes * scale).reshape(v.shape), -1, axis)


WIDE = False


def mx_kscale(k):
    if not WIDE:
        return np.ones(k)
    levels = np.array([10, -10, 5, -5, 0])
    if k % 512:
        return np.exp2(np.random.permutation(np.resize(levels, k // 32))).repeat(32)
    a = np.empty((k // 512, 16))
    for p in range(k // 512):
        a[p, :8] = np.random.permutation(np.resize(levels, 8))
        for g in range(8):
            far = levels[np.abs(levels - a[p, g]) >= 10]
            a[p, g + 8] = far[np.random.randint(len(far))]
    return np.exp2(a.ravel()).repeat(32)


BF16 = ml_dtypes.bfloat16


def bf(x):
    return np.asarray(x, np.float32).astype(BF16)


def f64(x):
    return np.asarray(x).astype(np.float64)


B, L, D, O = 4, 128, 512, 32


def setup_inputs():
    s = mx_kscale(D)
    u = mx_kscale(D)
    w = np.random.standard_normal((O, D + 1, D))
    w[:, :D, :] *= 3.0 / D / s[:, None]
    w[:, D, :] *= 1.0 / np.sqrt(D)
    return {"x1": bf(np.random.standard_normal((B, L, D)) * s),
            "x2": bf(np.random.standard_normal((B, L, D)) / u),
            "bw": bf(np.random.uniform(size=(2,))),
            "W_bil": bf(w * u),
            "t_ones": bf(np.random.standard_normal((B, L, O))),
            "lin1": bf(np.random.standard_normal((B, L, O))),
            "lin2": bf(np.random.standard_normal((B, L, O))),
            "b_lin": bf(np.random.standard_normal(O) * 0.5)}


def reference(x1, x2, bw, W_bil, t_ones, lin1, lin2, b_lin):
    e = np.exp(f64(bw) - f64(bw).max())
    bwn = e / e.sum()
    w = f64(W_bil)
    t = (mxq(f64(x1).reshape(B * L, D), 1, "e4m3") @ mxq(w[:, :D, :], 1, "e4m3")) + w[:, D, :][:, None, :]
    t = t.reshape(O, B, L, D)
    pair = mxq(t, 3, "e4m3") @ mxq(f64(x2), 2, "e4m3").transpose(0, 2, 1)
    bil = pair.transpose(1, 2, 3, 0) + f64(t_ones)[:, :, None, :]
    lin = f64(lin1)[:, :, None, :] + f64(lin2)[:, None, :, :] + f64(b_lin)
    return bwn[0] * bil + bwn[1] * lin

@@ -1,0 +1,243 @@
+from contextlib import ExitStack
+
+import concourse.mybir as mybir
+from concourse.masks import make_identity
+
+B, L, D, O = 4, 128, 512, 32
+FLOPS = 2 * (B * L) * D * (O * D) + 2 * O * B * L * L * D
+
+F32 = mybir.dt.float32
+BF16 = mybir.dt.bfloat16
+U32 = mybir.dt.uint32
+U8 = mybir.dt.uint8
+FP8X4 = mybir.dt.float8_e4m3fn_x4
+ACT = mybir.ActivationFunctionType
+ALU = mybir.AluOpType
+
+P = 128
+PACK = 4
+N1 = B * L
+NV = 304
+BANK_DT = F32
+
+
+def tile_biaffine_pa_kernel(tc, x1, x2, bw, W_bil, t_ones, lin1, lin2, b_lin, out):
+    nc = tc.nc
+    with ExitStack() as ctx:
+        keep = ctx.enter_context(tc.tile_pool(name="keep", bufs=1))
+        psum = ctx.enter_context(tc.psum_pool(name="psum", bufs=8))
+        ctx.enter_context(tc.manual_schedule())
+
+        ident = keep.tile([P, P], F32, name="ident")
+        x1c = keep.tile([P, N1], U32, name="x1c", align_bytes=64)
+        x1s = keep.tile([P, N1], U8, name="x1s", align_bytes=64)
+        x2c = keep.tile([P, N1], U32, name="x2c", align_bytes=64)
+        x2s = keep.tile([P, N1], U8, name="x2s", align_bytes=64)
+        bias = keep.tile([P, O, PACK], BF16, name="bias")
+        lin2b = keep.tile([P, B, L, O], BF16, name="lin2b")
+        tcod = [keep.tile([P, N1], U32, name="tcod%d" % o, align_bytes=64) for o in range(O)]
+        tsc = [keep.tile([P, N1], U8, name="tsc%d" % o, align_bytes=64) for o in range(O)]
+        bw_b = keep.tile([P, 2], BF16, name="bw_b")
+        bwf = keep.tile([P, 2], F32, name="bwf")
+        bwmax = keep.tile([P, 1], F32, name="bwmax")
+        bwd = keep.tile([P, 2], F32, name="bwd")
+        bwe = keep.tile([P, 2], F32, name="bwe")
+        bwsum = keep.tile([P, 1], F32, name="bwsum")
+        bwrec = keep.tile([P, 1], F32, name="bwrec")
+        bwn = keep.tile([P, 2], F32, name="bwn")
+        blin = keep.tile([P, O], BF16, name="blin")
+        tones = keep.tile([P, B, O], BF16, name="tones")
+        lin1s = keep.tile([P, B, O], BF16, name="lin1s")
+        xsum = keep.tile([P, B, O], F32, name="xsum")
+        xscl = keep.tile([P, B, O], F32, name="xscl")
+        xterm = keep.tile([P, B, O], F32, name="xterm")
+
+        with ExitStack() as ph1:
+            prep = ph1.enter_context(tc.tile_pool(name="prep", bufs=1))
+            rawp = ph1.enter_context(tc.tile_pool(name="rawp", bufs=4))
+            wgp = ph1.enter_context(tc.tile_pool(name="wgp", bufs=2))
+            wcp = ph1.enter_context(tc.tile_pool(name="wcp", bufs=4))
+            tbp = ph1.enter_context(tc.tile_pool(name="tbp", bufs=4))
+            tgp = ph1.enter_context(tc.tile_pool(name="tgp", bufs=4))
+
+            raw = {}
+            wg = {}
+            wc = {}
+            ws = {}
+            tb = {}
+            tg = {}
+            banks = {}
+
+            def load_w(o):
+                raw[o] = rawp.tile([P, PACK, D], BF16, name="raw")
+                nc.sync.dma_start(out=raw[o][:], in_=W_bil[o, 0:D, :].rearrange("(p j) c -> p j c", j=PACK))
+
+            def w_interleave(o):
+                wg[o] = wgp.tile([P, PACK * D], BF16, name="wg", align_bytes=64)
+                nc.vector.tensor_copy(
+                    out=wg[o][:].rearrange("p (t m j) -> p t m j", t=PACK, j=PACK),
+                    in_=raw[o][:].rearrange("p j (m t) -> p t m j", t=PACK),
+                )
+
+            def w_quantize(o):
+                wc[o] = wcp.tile([P, D], U32, name="wc", align_bytes=64)
+                ws[o] = wcp.tile([P, D], U8, name="ws", align_bytes=64)
+                nc.vector.quantize_mx(out=wc[o][:].bitcast(FP8X4), scales=ws[o][:], in_=wg[o][:])
+
+            def stage1_matmuls(o):
+                banks[o] = []
+                for t in range(PACK):
+                    cols = slice(P * t, P * (t + 1))
+                    bank = psum.tile([P, N1], BANK_DT, tag="bank", name="s1bank")
+                    nc.tensor.matmul_mx(
+                        out=bank[:],
+                        lhsT=wc[o][:, cols].bitcast(FP8X4),
+                        lhsT_scale=ws[o][:, cols],
+                        rhs=x1c[:].bitcast(FP8X4),
+                        rhs_scale=x1s[:],
+                        start=True,
+                        stop=True,
+                    )
+                    banks[o].append(bank)
+
+            def stage1_read(o):
+                tb[o] = tbp.tile([P, PACK, N1], BF16, name="tb")
+                for t in range(PACK):
+                    nc.scalar.activation(
+                        out=tb[o][:, t, :],
+                        in_=banks[o][t][:],
+                        func=ACT.Identity,
+                        bias=bias[:, o, t : t + 1],
+                        scale=1.0,
+                    )
+
+            def t_interleave_scalar(o):
+                tg[o] = tgp.tile([P, N1, PACK], BF16, name="tg", align_bytes=64)
+                nc.scalar.copy(out=tg[o][:, NV:N1, :], in_=tb[o][:, :, NV:N1].rearrange("p t n -> p n t"))
+
+            def t_interleave_vector(o):
+                nc.vector.tensor_copy(out=tg[o][:, 0:NV, :], in_=tb[o][:, :, 0:NV].rearrange("p t n -> p n t"))
+
+            def t_quantize(o):
+                nc.vector.quantize_mx(
+                    out=tcod[o][:].bitcast(FP8X4), scales=tsc[o][:], in_=tg[o][:].rearrange("p n t -> p (n t)")
+                )
+
+            def turn_rows(rows, grouped):
+                words = rows[:].rearrange("p b i -> p (b i)").bitcast(F32)
+                gwords = grouped[:].rearrange("p n j -> p (n j)").bitcast(F32)
+                for h in range(2):
+                    xt = psum.tile([P, 2, 2, L], F32, tag="bank", name="xt")
+                    for bb in range(2):
+                        b = 2 * h + bb
+                        for u in range(2):
+                            nc.tensor.transpose(
+                                xt[:, bb, u, :], words[:, 256 * b + u : 256 * (b + 1) : 2], ident[:]
+                            )
+                    nc.scalar.copy(
+                        out=gwords[:, 512 * h : 512 * (h + 1)].rearrange("p (bb x u) -> p bb x u", bb=2, u=2),
+                        in_=xt[:].rearrange("p bb u x -> p bb x u"),
+                    )
+
+            x1r = prep.tile([P, B, D], BF16, name="x1r")
+            x2r = prep.tile([P, B, D], BF16, name="x2r")
+            x1g = prep.tile([P, N1, PACK], BF16, name="x1g", align_bytes=64)
+            x2g = prep.tile([P, N1, PACK], BF16, name="x2g", align_bytes=64)
+            nc.sync.dma_start(out=x1r[:], in_=x1.rearrange("b x i -> x b i"))
+            for o in range(3):
+                load_w(o)
+            make_identity(nc, ident[:])
+            nc.scalar.dma_start(out=bw_b[:], in_=bw.partition_broadcast(P))
+            nc.scalar.dma_start(out=bias[:, 0:8, :], in_=W_bil[0:8, D, :].rearrange("o (p t) -> p o t", t=PACK))
+            nc.scalar.dma_start(out=x2r[:], in_=x2.rearrange("b x i -> x b i"))
+            nc.scalar.dma_start(out=bias[:, 8:O, :], in_=W_bil[8:O, D, :].rearrange("o (p t) -> p o t", t=PACK))
+            nc.scalar.dma_start(out=blin[:], in_=b_lin.partition_broadcast(P))
+            nc.scalar.dma_start(out=tones[:], in_=t_ones.rearrange("b x o -> x b o"))
+            nc.scalar.dma_start(out=lin1s[:], in_=lin1.rearrange("b x o -> x b o"))
+
+            nc.vector.tensor_copy(out=bwf[:], in_=bw_b[:])
+            nc.vector.tensor_tensor(out=bwmax[:], in0=bwf[:, 0:1], in1=bwf[:, 1:2], op=ALU.max)
+            nc.vector.tensor_scalar(out=bwd[:], in0=bwf[:], scalar1=bwmax[:, 0:1], scalar2=None, op0=ALU.subtract)
+            nc.scalar.activation(out=bwe[:], in_=bwd[:], func=ACT.Exp)
+
+            turn_rows(x1r, x1g)
+            turn_rows(x2r, x2g)
+
+            for i in range(-2, O + 4):
+                if 0 <= i + 5 < O and i + 5 >= 3:
+                    load_w(i + 5)
+                if 0 <= i < B:
+                    nc.sync.dma_start(
+                        out=lin2b[:, i, :, :].rearrange("p y o -> p (y o)"),
+                        in_=lin2[i].rearrange("y o -> (y o)").partition_broadcast(P),
+                    )
+                if i + 2 < O:
+                    w_interleave(i + 2)
+                if i == -2:
+                    nc.vector.quantize_mx(
+                        out=x1c[:].bitcast(FP8X4), scales=x1s[:], in_=x1g[:].rearrange("p n j -> p (n j)")
+                    )
+                if i == 1:
+                    nc.vector.quantize_mx(
+                        out=x2c[:].bitcast(FP8X4), scales=x2s[:], in_=x2g[:].rearrange("p n j -> p (n j)")
+                    )
+                if 0 <= i - 3 < O:
+                    t_quantize(i - 3)
+                if 0 <= i - 2 < O:
+                    t_interleave_vector(i - 2)
+                if i + 2 < O:
+                    w_quantize(i + 2)
+                if i == 2:
+                    nc.vector.tensor_tensor(out=bwsum[:], in0=bwe[:, 0:1], in1=bwe[:, 1:2], op=ALU.add)
+                    nc.vector.reciprocal(out=bwrec[:], in_=bwsum[:])
+                    nc.vector.tensor_scalar(out=bwn[:], in0=bwe[:], scalar1=bwrec[:, 0:1], scalar2=None, op0=ALU.mult)
+                    for b in range(B):
+                        nc.vector.tensor_tensor(out=xsum[:, b, :], in0=lin1s[:, b, :], in1=blin[:], op=ALU.add)
+                    nc.vector.tensor_scalar(out=xscl[:], in0=xsum[:], scalar1=bwn[:, 1:2], scalar2=None, op0=ALU.mult)
+                    nc.vector.scalar_tensor_tensor(
+                        out=xterm[:], in0=tones[:], scalar=bwn[:, 0:1], in1=xscl[:], op0=ALU.mult, op1=ALU.add
+                    )
+                if 0 <= i + 1 < O:
+                    stage1_matmuls(i + 1)
+                if 0 <= i - 1 < O:
+                    t_interleave_scalar(i - 1)
+                if 0 <= i < O:
+                    stage1_read(i)
+
+        stp = ctx.enter_context(tc.tile_pool(name="stp", bufs=4))
+        tmpp = ctx.enter_context(tc.tile_pool(name="tmpp", bufs=6))
+        for b in range(B):
+            cols = slice(L * b, L * (b + 1))
+            stage = stp.tile([P, L, O], F32, name="stage")
+            for g in range(O // 4):
+                pair = psum.tile([P, 4, L], F32, tag="bank", name="pair")
+                for q in range(4):
+                    o = 4 * g + q
+                    nc.tensor.matmul_mx(
+                        out=pair[:, q, :],
+                        lhsT=tcod[o][:, cols].bitcast(FP8X4),
+                        lhsT_scale=tsc[o][:, cols],
+                        rhs=x2c[:, cols].bitcast(FP8X4),
+                        rhs_scale=x2s[:, cols],
+                        start=True,
+                        stop=True,
+                    )
+                tmp = tmpp.tile([P, 4, L], F32, name="tmp")
+                for q in range(4):
+                    o = 4 * g + q
+                    nc.scalar.activation(
+                        out=tmp[:, q, :],
+                        in_=pair[:, q, :],
+                        func=ACT.Identity,
+                        bias=xterm[:, b, o : o + 1],
+                        scale=bwn[:, 0:1],
+                    )
+                nc.vector.scalar_tensor_tensor(
+                    out=stage[:, :, 4 * g : 4 * g + 4],
+                    in0=lin2b[:, b, :, 4 * g : 4 * g + 4],
+                    scalar=bwn[:, 1:2],
+                    in1=tmp[:].rearrange("p q y -> p y q"),
+                    op0=ALU.mult,
+                    op1=ALU.add,
+                )
+            nc.sync.dma_start(out=out[b].rearrange("x y o -> x (y o)"), in_=stage[:].rearrange("p y o -> p (y o)"))

@@ -17,7 +17,8 @@ ALU = mybir.AluOpType
 P = 128
 PACK = 4
 N1 = B * L
-NV = 304
+MH = 64
+O_PE = 31
 BANK_DT = F32
 
 
@@ -29,6 +30,7 @@ def tile_biaffine_pa_kernel(tc, x1, x2, bw, W_bil, t_ones, lin1, lin2, b_lin, ou
         ctx.enter_context(tc.manual_schedule())
 
         ident = keep.tile([P, P], F32, name="ident")
+        identb = keep.tile([P, P], BF16, name="identb")
         x1c = keep.tile([P, N1], U32, name="x1c", align_bytes=64)
         x1s = keep.tile([P, N1], U8, name="x1s", align_bytes=64)
         x2c = keep.tile([P, N1], U32, name="x2c", align_bytes=64)
@@ -54,8 +56,8 @@ def tile_biaffine_pa_kernel(tc, x1, x2, bw, W_bil, t_ones, lin1, lin2, b_lin, ou
 
         with ExitStack() as ph1:
             prep = ph1.enter_context(tc.tile_pool(name="prep", bufs=1))
-            rawp = ph1.enter_context(tc.tile_pool(name="rawp", bufs=4))
-            wgp = ph1.enter_context(tc.tile_pool(name="wgp", bufs=2))
+            rawp = ph1.enter_context(tc.tile_pool(name="rawp", bufs=5))
+            wgp = ph1.enter_context(tc.tile_pool(name="wgp", bufs=3))
             wcp = ph1.enter_context(tc.tile_pool(name="wcp", bufs=4))
             tbp = ph1.enter_context(tc.tile_pool(name="tbp", bufs=4))
             tgp = ph1.enter_context(tc.tile_pool(name="tgp", bufs=4))
@@ -72,11 +74,30 @@ def tile_biaffine_pa_kernel(tc, x1, x2, bw, W_bil, t_ones, lin1, lin2, b_lin, ou
                 raw[o] = rawp.tile([P, PACK, D], BF16, name="raw")
                 nc.sync.dma_start(out=raw[o][:], in_=W_bil[o, 0:D, :].rearrange("(p j) c -> p j c", j=PACK))
 
-            def w_interleave(o):
+            def w_interleave_tensor(o):
                 wg[o] = wgp.tile([P, PACK * D], BF16, name="wg", align_bytes=64)
+                wid = psum.tile([P, PACK, MH, PACK], BF16, tag="bank", name="wid")
+                for h in range(2):
+                    nc.tensor.matmul(
+                        out=wid[:, 2 * h : 2 * h + 2, :, :],
+                        lhsT=identb[:],
+                        rhs=raw[o][:].rearrange("p j (m t) -> p t m j", t=PACK)[:, 2 * h : 2 * h + 2, MH:P, :],
+                        start=True,
+                        stop=True,
+                    )
+                nc.scalar.copy(
+                    out=wg[o][:].rearrange("p (t m j) -> p t m j", t=PACK, j=PACK)[:, :, MH:P, :], in_=wid[:]
+                )
+
+            def w_interleave_vector(o):
+                if o < O_PE:
+                    mv = MH
+                else:
+                    mv = P
+                    wg[o] = wgp.tile([P, PACK * D], BF16, name="wg", align_bytes=64)
                 nc.vector.tensor_copy(
-                    out=wg[o][:].rearrange("p (t m j) -> p t m j", t=PACK, j=PACK),
-                    in_=raw[o][:].rearrange("p j (m t) -> p t m j", t=PACK),
+                    out=wg[o][:].rearrange("p (t m j) -> p m j t", t=PACK, j=PACK)[:, 0:mv, :, :],
+                    in_=raw[o][:].rearrange("p j (m t) -> p m j t", t=PACK)[:, 0:mv, :, :],
                 )
 
             def w_quantize(o):
@@ -84,39 +105,37 @@ def tile_biaffine_pa_kernel(tc, x1, x2, bw, W_bil, t_ones, lin1, lin2, b_lin, ou
                 ws[o] = wcp.tile([P, D], U8, name="ws", align_bytes=64)
                 nc.vector.quantize_mx(out=wc[o][:].bitcast(FP8X4), scales=ws[o][:], in_=wg[o][:])
 
-            def stage1_matmuls(o):
-                banks[o] = []
-                for t in range(PACK):
-                    cols = slice(P * t, P * (t + 1))
-                    bank = psum.tile([P, N1], BANK_DT, tag="bank", name="s1bank")
-                    nc.tensor.matmul_mx(
-                        out=bank[:],
-                        lhsT=wc[o][:, cols].bitcast(FP8X4),
-                        lhsT_scale=ws[o][:, cols],
-                        rhs=x1c[:].bitcast(FP8X4),
-                        rhs_scale=x1s[:],
-                        start=True,
-                        stop=True,
-                    )
-                    banks[o].append(bank)
+            def stage1_matmul(o, t):
+                cols = slice(P * t, P * (t + 1))
+                bank = psum.tile([P, N1], BANK_DT, tag="bank", name="s1bank")
+                nc.tensor.matmul_mx(
+                    out=bank[:],
+                    lhsT=wc[o][:, cols].bitcast(FP8X4),
+                    lhsT_scale=ws[o][:, cols],
+                    rhs=x1c[:].bitcast(FP8X4),
+                    rhs_scale=x1s[:],
+                    start=True,
+                    stop=True,
+                )
+                banks[(o, t)] = bank
 
-            def stage1_read(o):
-                tb[o] = tbp.tile([P, PACK, N1], BF16, name="tb")
-                for t in range(PACK):
-                    nc.scalar.activation(
-                        out=tb[o][:, t, :],
-                        in_=banks[o][t][:],
-                        func=ACT.Identity,
-                        bias=bias[:, o, t : t + 1],
-                        scale=1.0,
-                    )
+            def stage1_read(o, t):
+                if t == 0:
+                    tb[o] = tbp.tile([P, PACK, N1], BF16, name="tb")
+                nc.scalar.activation(
+                    out=tb[o][:, t, :],
+                    in_=banks[(o, t)][:],
+                    func=ACT.Identity,
+                    bias=bias[:, o, t : t + 1],
+                    scale=1.0,
+                )
 
-            def t_interleave_scalar(o):
+            def t_interleave(o):
                 tg[o] = tgp.tile([P, N1, PACK], BF16, name="tg", align_bytes=64)
-                nc.scalar.copy(out=tg[o][:, NV:N1, :], in_=tb[o][:, :, NV:N1].rearrange("p t n -> p n t"))
-
-            def t_interleave_vector(o):
-                nc.vector.tensor_copy(out=tg[o][:, 0:NV, :], in_=tb[o][:, :, 0:NV].rearrange("p t n -> p n t"))
+                nc.vector.tensor_copy(
+                    out=tg[o][:].rearrange("p (c i) t -> p c t i", i=4),
+                    in_=tb[o][:].rearrange("p t (c i) -> p c t i", i=4),
+                )
 
             def t_quantize(o):
                 nc.vector.quantize_mx(
@@ -147,13 +166,10 @@ def tile_biaffine_pa_kernel(tc, x1, x2, bw, W_bil, t_ones, lin1, lin2, b_lin, ou
             for o in range(3):
                 load_w(o)
             make_identity(nc, ident[:])
+            make_identity(nc, identb[:])
             nc.scalar.dma_start(out=bw_b[:], in_=bw.partition_broadcast(P))
             nc.scalar.dma_start(out=bias[:, 0:8, :], in_=W_bil[0:8, D, :].rearrange("o (p t) -> p o t", t=PACK))
             nc.scalar.dma_start(out=x2r[:], in_=x2.rearrange("b x i -> x b i"))
-            nc.scalar.dma_start(out=bias[:, 8:O, :], in_=W_bil[8:O, D, :].rearrange("o (p t) -> p o t", t=PACK))
-            nc.scalar.dma_start(out=blin[:], in_=b_lin.partition_broadcast(P))
-            nc.scalar.dma_start(out=tones[:], in_=t_ones.rearrange("b x o -> x b o"))
-            nc.scalar.dma_start(out=lin1s[:], in_=lin1.rearrange("b x o -> x b o"))
 
             nc.vector.tensor_copy(out=bwf[:], in_=bw_b[:])
             nc.vector.tensor_tensor(out=bwmax[:], in0=bwf[:, 0:1], in1=bwf[:, 1:2], op=ALU.max)
@@ -161,18 +177,29 @@ def tile_biaffine_pa_kernel(tc, x1, x2, bw, W_bil, t_ones, lin1, lin2, b_lin, ou
             nc.scalar.activation(out=bwe[:], in_=bwd[:], func=ACT.Exp)
 
             turn_rows(x1r, x1g)
-            turn_rows(x2r, x2g)
 
-            for i in range(-2, O + 4):
-                if 0 <= i + 5 < O and i + 5 >= 3:
-                    load_w(i + 5)
-                if 0 <= i < B:
-                    nc.sync.dma_start(
-                        out=lin2b[:, i, :, :].rearrange("p y o -> p (y o)"),
-                        in_=lin2[i].rearrange("y o -> (y o)").partition_broadcast(P),
+            for i in range(-3, O + 3):
+                if 3 <= i + 6 < O:
+                    load_w(i + 6)
+                if i == 0:
+                    nc.scalar.dma_start(
+                        out=bias[:, 8:O, :], in_=W_bil[8:O, D, :].rearrange("o (p t) -> p o t", t=PACK)
                     )
-                if i + 2 < O:
-                    w_interleave(i + 2)
+                    nc.scalar.dma_start(out=blin[:], in_=b_lin.partition_broadcast(P))
+                    nc.scalar.dma_start(out=tones[:], in_=t_ones.rearrange("b x o -> x b o"))
+                    nc.scalar.dma_start(out=lin1s[:], in_=lin1.rearrange("b x o -> x b o"))
+                if i >= 6 and i % 4 == 2 and (i - 6) // 4 < B:
+                    b = (i - 6) // 4
+                    nc.sync.dma_start(
+                        out=lin2b[:, b, :, :].rearrange("p y o -> p (y o)"),
+                        in_=lin2[b].rearrange("y o -> (y o)").partition_broadcast(P),
+                    )
+                if i + 3 < O_PE:
+                    w_interleave_tensor(i + 3)
+                if i == -1:
+                    turn_rows(x2r, x2g)
+                if 0 <= i + 2 < O:
+                    w_interleave_vector(i + 2)
                 if i == -2:
                     nc.vector.quantize_mx(
                         out=x1c[:].bitcast(FP8X4), scales=x1s[:], in_=x1g[:].rearrange("p n j -> p (n j)")
@@ -184,10 +211,10 @@ def tile_biaffine_pa_kernel(tc, x1, x2, bw, W_bil, t_ones, lin1, lin2, b_lin, ou
                 if 0 <= i - 3 < O:
                     t_quantize(i - 3)
                 if 0 <= i - 2 < O:
-                    t_interleave_vector(i - 2)
-                if i + 2 < O:
+                    t_interleave(i - 2)
+                if 0 <= i + 2 < O:
                     w_quantize(i + 2)
-                if i == 2:
+                if i == 4:
                     nc.vector.tensor_tensor(out=bwsum[:], in0=bwe[:, 0:1], in1=bwe[:, 1:2], op=ALU.add)
                     nc.vector.reciprocal(out=bwrec[:], in_=bwsum[:])
                     nc.vector.tensor_scalar(out=bwn[:], in0=bwe[:], scalar1=bwrec[:, 0:1], scalar2=None, op0=ALU.mult)
@@ -197,12 +224,11 @@ def tile_biaffine_pa_kernel(tc, x1, x2, bw, W_bil, t_ones, lin1, lin2, b_lin, ou
                     nc.vector.scalar_tensor_tensor(
                         out=xterm[:], in0=tones[:], scalar=bwn[:, 0:1], in1=xscl[:], op0=ALU.mult, op1=ALU.add
                     )
-                if 0 <= i + 1 < O:
-                    stage1_matmuls(i + 1)
-                if 0 <= i - 1 < O:
-                    t_interleave_scalar(i - 1)
-                if 0 <= i < O:
-                    stage1_read(i)
+                for t in range(PACK):
+                    if 0 <= i < O:
+                        stage1_read(i, t)
+                    if 0 <= i + 1 < O:
+                        stage1_matmul(i + 1, t)
 
         stp = ctx.enter_context(tc.tile_pool(name="stp", bufs=4))
         tmpp = ctx.enter_context(tc.tile_pool(name="tmpp", bufs=6))

@@ -19,6 +19,7 @@ PACK = 4
 N1 = B * L
 MH = 64
 O_PE = 31
+T_SCALAR = 3
 BANK_DT = F32
 
 
@@ -122,13 +123,22 @@ def tile_biaffine_pa_kernel(tc, x1, x2, bw, W_bil, t_ones, lin1, lin2, b_lin, ou
             def stage1_read(o, t):
                 if t == 0:
                     tb[o] = tbp.tile([P, PACK, N1], BF16, name="tb")
-                nc.scalar.activation(
-                    out=tb[o][:, t, :],
-                    in_=banks[(o, t)][:],
-                    func=ACT.Identity,
-                    bias=bias[:, o, t : t + 1],
-                    scale=1.0,
-                )
+                if t < T_SCALAR:
+                    nc.scalar.activation(
+                        out=tb[o][:, t, :],
+                        in_=banks[(o, t)][:],
+                        func=ACT.Identity,
+                        bias=bias[:, o, t : t + 1],
+                        scale=1.0,
+                    )
+                else:
+                    nc.vector.tensor_scalar(
+                        out=tb[o][:, t, :],
+                        in0=banks[(o, t)][:],
+                        scalar1=bias[:, o, t : t + 1],
+                        scalar2=None,
+                        op0=ALU.add,
+                    )
 
             def t_interleave(o):
                 tg[o] = tgp.tile([P, N1, PACK], BF16, name="tg", align_bytes=64)

from contextlib import ExitStack

import concourse.mybir as mybir
from concourse.masks import make_identity

B, L, D, O = 4, 128, 512, 32
FLOPS = 2 * (B * L) * D * (O * D) + 2 * O * B * L * L * D

F32 = mybir.dt.float32
BF16 = mybir.dt.bfloat16
U32 = mybir.dt.uint32
U8 = mybir.dt.uint8
FP8X4 = mybir.dt.float8_e4m3fn_x4
ACT = mybir.ActivationFunctionType
ALU = mybir.AluOpType

P = 128
PACK = 4
N1 = B * L
MH = 64
O_PE = 31
T_SCALAR = 3
BANK_DT = F32


def tile_biaffine_pa_kernel(tc, x1, x2, bw, W_bil, t_ones, lin1, lin2, b_lin, out):
    nc = tc.nc
    with ExitStack() as ctx:
        keep = ctx.enter_context(tc.tile_pool(name="keep", bufs=1))
        psum = ctx.enter_context(tc.psum_pool(name="psum", bufs=8))
        ctx.enter_context(tc.manual_schedule())

        ident = keep.tile([P, P], F32, name="ident")
        identb = keep.tile([P, P], BF16, name="identb")
        x1c = keep.tile([P, N1], U32, name="x1c", align_bytes=64)
        x1s = keep.tile([P, N1], U8, name="x1s", align_bytes=64)
        x2c = keep.tile([P, N1], U32, name="x2c", align_bytes=64)
        x2s = keep.tile([P, N1], U8, name="x2s", align_bytes=64)
        bias = keep.tile([P, O, PACK], BF16, name="bias")
        lin2b = keep.tile([P, B, L, O], BF16, name="lin2b")
        tcod = [keep.tile([P, N1], U32, name="tcod%d" % o, align_bytes=64) for o in range(O)]
        tsc = [keep.tile([P, N1], U8, name="tsc%d" % o, align_bytes=64) for o in range(O)]
        bw_b = keep.tile([P, 2], BF16, name="bw_b")
        bwf = keep.tile([P, 2], F32, name="bwf")
        bwmax = keep.tile([P, 1], F32, name="bwmax")
        bwd = keep.tile([P, 2], F32, name="bwd")
        bwe = keep.tile([P, 2], F32, name="bwe")
        bwsum = keep.tile([P, 1], F32, name="bwsum")
        bwrec = keep.tile([P, 1], F32, name="bwrec")
        bwn = keep.tile([P, 2], F32, name="bwn")
        blin = keep.tile([P, O], BF16, name="blin")
        tones = keep.tile([P, B, O], BF16, name="tones")
        lin1s = keep.tile([P, B, O], BF16, name="lin1s")
        xsum = keep.tile([P, B, O], F32, name="xsum")
        xscl = keep.tile([P, B, O], F32, name="xscl")
        xterm = keep.tile([P, B, O], F32, name="xterm")

        with ExitStack() as ph1:
            prep = ph1.enter_context(tc.tile_pool(name="prep", bufs=1))
            rawp = ph1.enter_context(tc.tile_pool(name="rawp", bufs=5))
            wgp = ph1.enter_context(tc.tile_pool(name="wgp", bufs=3))
            wcp = ph1.enter_context(tc.tile_pool(name="wcp", bufs=4))
            tbp = ph1.enter_context(tc.tile_pool(name="tbp", bufs=4))
            tgp = ph1.enter_context(tc.tile_pool(name="tgp", bufs=4))

            raw = {}
            wg = {}
            wc = {}
            ws = {}
            tb = {}
            tg = {}
            banks = {}

            def load_w(o):
                raw[o] = rawp.tile([P, PACK, D], BF16, name="raw")
                nc.sync.dma_start(out=raw[o][:], in_=W_bil[o, 0:D, :].rearrange("(p j) c -> p j c", j=PACK))

            def w_interleave_tensor(o):
                wg[o] = wgp.tile([P, PACK * D], BF16, name="wg", align_bytes=64)
                wid = psum.tile([P, PACK, MH, PACK], BF16, tag="bank", name="wid")
                for h in range(2):
                    nc.tensor.matmul(
                        out=wid[:, 2 * h : 2 * h + 2, :, :],
                        lhsT=identb[:],
                        rhs=raw[o][:].rearrange("p j (m t) -> p t m j", t=PACK)[:, 2 * h : 2 * h + 2, MH:P, :],
                        start=True,
                        stop=True,
                    )
                nc.scalar.copy(
                    out=wg[o][:].rearrange("p (t m j) -> p t m j", t=PACK, j=PACK)[:, :, MH:P, :], in_=wid[:]
                )

            def w_interleave_vector(o):
                if o < O_PE:
                    mv = MH
                else:
                    mv = P
                    wg[o] = wgp.tile([P, PACK * D], BF16, name="wg", align_bytes=64)
                nc.vector.tensor_copy(
                    out=wg[o][:].rearrange("p (t m j) -> p m j t", t=PACK, j=PACK)[:, 0:mv, :, :],
                    in_=raw[o][:].rearrange("p j (m t) -> p m j t", t=PACK)[:, 0:mv, :, :],
                )

            def w_quantize(o):
                wc[o] = wcp.tile([P, D], U32, name="wc", align_bytes=64)
                ws[o] = wcp.tile([P, D], U8, name="ws", align_bytes=64)
                nc.vector.quantize_mx(out=wc[o][:].bitcast(FP8X4), scales=ws[o][:], in_=wg[o][:])

            def stage1_matmul(o, t):
                cols = slice(P * t, P * (t + 1))
                bank = psum.tile([P, N1], BANK_DT, tag="bank", name="s1bank")
                nc.tensor.matmul_mx(
                    out=bank[:],
                    lhsT=wc[o][:, cols].bitcast(FP8X4),
                    lhsT_scale=ws[o][:, cols],
                    rhs=x1c[:].bitcast(FP8X4),
                    rhs_scale=x1s[:],
                    start=True,
                    stop=True,
                )
                banks[(o, t)] = bank

            def stage1_read(o, t):
                if t == 0:
                    tb[o] = tbp.tile([P, PACK, N1], BF16, name="tb")
                if t < T_SCALAR:
                    nc.scalar.activation(
                        out=tb[o][:, t, :],
                        in_=banks[(o, t)][:],
                        func=ACT.Identity,
                        bias=bias[:, o, t : t + 1],
                        scale=1.0,
                    )
                else:
                    nc.vector.tensor_scalar(
                        out=tb[o][:, t, :],
                        in0=banks[(o, t)][:],
                        scalar1=bias[:, o, t : t + 1],
                        scalar2=None,
                        op0=ALU.add,
                    )

            def t_interleave(o):
                tg[o] = tgp.tile([P, N1, PACK], BF16, name="tg", align_bytes=64)
                nc.vector.tensor_copy(
                    out=tg[o][:].rearrange("p (c i) t -> p c t i", i=4),
                    in_=tb[o][:].rearrange("p t (c i) -> p c t i", i=4),
                )

            def t_quantize(o):
                nc.vector.quantize_mx(
                    out=tcod[o][:].bitcast(FP8X4), scales=tsc[o][:], in_=tg[o][:].rearrange("p n t -> p (n t)")
                )

            def turn_rows(rows, grouped):
                words = rows[:].rearrange("p b i -> p (b i)").bitcast(F32)
                gwords = grouped[:].rearrange("p n j -> p (n j)").bitcast(F32)
                for h in range(2):
                    xt = psum.tile([P, 2, 2, L], F32, tag="bank", name="xt")
                    for bb in range(2):
                        b = 2 * h + bb
                        for u in range(2):
                            nc.tensor.transpose(
                                xt[:, bb, u, :], words[:, 256 * b + u : 256 * (b + 1) : 2], ident[:]
                            )
                    nc.scalar.copy(
                        out=gwords[:, 512 * h : 512 * (h + 1)].rearrange("p (bb x u) -> p bb x u", bb=2, u=2),
                        in_=xt[:].rearrange("p bb u x -> p bb x u"),
                    )

            x1r = prep.tile([P, B, D], BF16, name="x1r")
            x2r = prep.tile([P, B, D], BF16, name="x2r")
            x1g = prep.tile([P, N1, PACK], BF16, name="x1g", align_bytes=64)
            x2g = prep.tile([P, N1, PACK], BF16, name="x2g", align_bytes=64)
            nc.sync.dma_start(out=x1r[:], in_=x1.rearrange("b x i -> x b i"))
            for o in range(3):
                load_w(o)
            make_identity(nc, ident[:])
            make_identity(nc, identb[:])
            nc.scalar.dma_start(out=bw_b[:], in_=bw.partition_broadcast(P))
            nc.scalar.dma_start(out=bias[:, 0:8, :], in_=W_bil[0:8, D, :].rearrange("o (p t) -> p o t", t=PACK))
            nc.scalar.dma_start(out=x2r[:], in_=x2.rearrange("b x i -> x b i"))

            nc.vector.tensor_copy(out=bwf[:], in_=bw_b[:])
            nc.vector.tensor_tensor(out=bwmax[:], in0=bwf[:, 0:1], in1=bwf[:, 1:2], op=ALU.max)
            nc.vector.tensor_scalar(out=bwd[:], in0=bwf[:], scalar1=bwmax[:, 0:1], scalar2=None, op0=ALU.subtract)
            nc.scalar.activation(out=bwe[:], in_=bwd[:], func=ACT.Exp)

            turn_rows(x1r, x1g)

            for i in range(-3, O + 3):
                if 3 <= i + 6 < O:
                    load_w(i + 6)
                if i == 0:
                    nc.scalar.dma_start(
                        out=bias[:, 8:O, :], in_=W_bil[8:O, D, :].rearrange("o (p t) -> p o t", t=PACK)
                    )
                    nc.scalar.dma_start(out=blin[:], in_=b_lin.partition_broadcast(P))
                    nc.scalar.dma_start(out=tones[:], in_=t_ones.rearrange("b x o -> x b o"))
                    nc.scalar.dma_start(out=lin1s[:], in_=lin1.rearrange("b x o -> x b o"))
                if i >= 6 and i % 4 == 2 and (i - 6) // 4 < B:
                    b = (i - 6) // 4
                    nc.sync.dma_start(
                        out=lin2b[:, b, :, :].rearrange("p y o -> p (y o)"),
                        in_=lin2[b].rearrange("y o -> (y o)").partition_broadcast(P),
                    )
                if i + 3 < O_PE:
                    w_interleave_tensor(i + 3)
                if i == -1:
                    turn_rows(x2r, x2g)
                if 0 <= i + 2 < O:
                    w_interleave_vector(i + 2)
                if i == -2:
                    nc.vector.quantize_mx(
                        out=x1c[:].bitcast(FP8X4), scales=x1s[:], in_=x1g[:].rearrange("p n j -> p (n j)")
                    )
                if i == 1:
                    nc.vector.quantize_mx(
                        out=x2c[:].bitcast(FP8X4), scales=x2s[:], in_=x2g[:].rearrange("p n j -> p (n j)")
                    )
                if 0 <= i - 3 < O:
                    t_quantize(i - 3)
                if 0 <= i - 2 < O:
                    t_interleave(i - 2)
                if 0 <= i + 2 < O:
                    w_quantize(i + 2)
                if i == 4:
                    nc.vector.tensor_tensor(out=bwsum[:], in0=bwe[:, 0:1], in1=bwe[:, 1:2], op=ALU.add)
                    nc.vector.reciprocal(out=bwrec[:], in_=bwsum[:])
                    nc.vector.tensor_scalar(out=bwn[:], in0=bwe[:], scalar1=bwrec[:, 0:1], scalar2=None, op0=ALU.mult)
                    for b in range(B):
                        nc.vector.tensor_tensor(out=xsum[:, b, :], in0=lin1s[:, b, :], in1=blin[:], op=ALU.add)
                    nc.vector.tensor_scalar(out=xscl[:], in0=xsum[:], scalar1=bwn[:, 1:2], scalar2=None, op0=ALU.mult)
                    nc.vector.scalar_tensor_tensor(
                        out=xterm[:], in0=tones[:], scalar=bwn[:, 0:1], in1=xscl[:], op0=ALU.mult, op1=ALU.add
                    )
                for t in range(PACK):
                    if 0 <= i < O:
                        stage1_read(i, t)
                    if 0 <= i + 1 < O:
                        stage1_matmul(i + 1, t)

        stp = ctx.enter_context(tc.tile_pool(name="stp", bufs=4))
        tmpp = ctx.enter_context(tc.tile_pool(name="tmpp", bufs=6))
        for b in range(B):
            cols = slice(L * b, L * (b + 1))
            stage = stp.tile([P, L, O], F32, name="stage")
            for g in range(O // 4):
                pair = psum.tile([P, 4, L], F32, tag="bank", name="pair")
                for q in range(4):
                    o = 4 * g + q
                    nc.tensor.matmul_mx(
                        out=pair[:, q, :],
                        lhsT=tcod[o][:, cols].bitcast(FP8X4),
                        lhsT_scale=tsc[o][:, cols],
                        rhs=x2c[:, cols].bitcast(FP8X4),
                        rhs_scale=x2s[:, cols],
                        start=True,
                        stop=True,
                    )
                tmp = tmpp.tile([P, 4, L], F32, name="tmp")
                for q in range(4):
                    o = 4 * g + q
                    nc.scalar.activation(
                        out=tmp[:, q, :],
                        in_=pair[:, q, :],
                        func=ACT.Identity,
                        bias=xterm[:, b, o : o + 1],
                        scale=bwn[:, 0:1],
                    )
                nc.vector.scalar_tensor_tensor(
                    out=stage[:, :, 4 * g : 4 * g + 4],
                    in0=lin2b[:, b, :, 4 * g : 4 * g + 4],
                    scalar=bwn[:, 1:2],
                    in1=tmp[:].rearrange("p q y -> p y q"),
                    op0=ALU.mult,
                    op1=ALU.add,
                )
            nc.sync.dma_start(out=out[b].rearrange("x y o -> x (y o)"), in_=stage[:].rearrange("p y o -> p (y o)"))
